import numpy as np
import ml_dtypes


def mxq(x, axis, fmt="e4m3"):
    dtype, down = {"e4m3": (ml_dtypes.float8_e4m3fn, 7), "e5m2": (ml_dtypes.float8_e5m2, 14)}[fmt]
    v = np.moveaxis(np.asarray(x, np.float32).astype(ml_dtypes.bfloat16).astype(np.float64), axis, -1)
    blocks = v.reshape(v.shape[:-1] + (-1, 32))
    amax = np.abs(blocks).max(-1, keepdims=True)
    byte = np.maximum(np.where(amax > 0, np.frexp(amax)[1] - 1 + 127, 0) - down, 1)
    scale = np.exp2(byte - 127.0)
    codes = (blocks / scale).astype(np.float32).astype(dtype).astype(np.float64)
    return np.moveaxis((codes * scale).reshape(v.shape), -1, axis)


WIDE = False


def mx_kscale(k):
    if not WIDE:
        return np.ones(k)
    levels = np.array([10, -10, 5, -5, 0])
    a = np.random.permutation(np.resize(levels, k // 512 * 4)).reshape(k // 512, 4)
    idx = np.arange(k)
    return np.exp2(a[idx // 512, idx % 128 // 32])


BF16 = ml_dtypes.bfloat16


def bf(x):
    return np.asarray(x, np.float32).astype(BF16)


def f64(x):
    return np.asarray(x).astype(np.float64)


NB, D1, KB, P, Q, LB, S = 4, 1024, 4, 1024, 128, 1, 128
D2 = KB * P
R = KB * Q // LB
DO = S * LB


def _blockdiag_butterfly_multiply(x, w1, w2):
    B, n = x.shape
    k, q, p = w1.shape
    l, s, r = w2.shape
    x_r = x.reshape(B, k, p).transpose(1, 0, 2)
    out1 = mxq(x_r, 2, "e4m3") @ mxq(w1, 2, "e4m3").transpose(0, 2, 1)
    out1 = out1.transpose(1, 0, 2).reshape(B, r, l).transpose(2, 0, 1)
    out2 = mxq(out1, 2, "e4m3") @ mxq(w2, 2, "e4m3").transpose(0, 2, 1)
    return out2.transpose(1, 2, 0).reshape(B, s * l)


def setup_inputs():
    s = mx_kscale(P)
    t = mx_kscale(R)
    tf = np.repeat(t, LB).reshape(KB, Q)
    return {"x": bf(np.random.standard_normal((NB, D1, D2)) * np.tile(s, KB)),
            "factorL": bf(np.random.standard_normal((KB, Q, P)) / np.sqrt(P) / s * tf[:, :, None]),
            "factorR": bf(np.random.standard_normal((LB, S, R)) / np.sqrt(R) / t),
            "bias": bf(np.random.standard_normal(DO) * 0.5)}


def reference(x, factorL, factorR, bias):
    b, d1, d2 = x.shape
    out = _blockdiag_butterfly_multiply(f64(x).reshape(-1, d2), f64(factorL), f64(factorR))
    out = out.reshape(b, d1, -1)
    return out + f64(bias)

@@ -1,0 +1,235 @@
+from contextlib import ExitStack
+
+import concourse.masks as masks
+import concourse.mybir as mybir
+
+FP8X4 = mybir.dt.float8_e4m3fn_x4
+BF16 = mybir.dt.bfloat16
+F32 = mybir.dt.float32
+U32 = mybir.dt.uint32
+U8 = mybir.dt.uint8
+
+P = 128
+ROWS = 4096
+COLS = 4096
+KB = 4
+TILES = ROWS // P
+GROUP = 4
+NGROUPS = TILES // GROUP
+UNIT = 2
+XBUFS = 4
+
+FLOPS = 2 * ROWS * COLS * 128 + 2 * ROWS * 512 * 128
+
+
+def tile_butterflyblocksparselinear_t_kernel(tc, x, factorL, factorR, bias, out):
+    nc = tc.nc
+    xg = x.flatten_outer_dims().rearrange("(g p t) c -> g p t c", p=P, t=GROUP)
+    og = out.flatten_outer_dims().rearrange("(g p t) s -> g p (t s)", p=P, t=GROUP)
+
+    with ExitStack() as ctx:
+        const = ctx.enter_context(tc.tile_pool(name="const", bufs=1))
+        xpool = ctx.enter_context(tc.tile_pool(name="xpool", bufs=XBUFS))
+        gpool = ctx.enter_context(tc.tile_pool(name="gpool", bufs=4))
+        cpool = ctx.enter_context(tc.tile_pool(name="cpool", bufs=4))
+        hpool = ctx.enter_context(tc.tile_pool(name="hpool", bufs=3))
+        opool = ctx.enter_context(tc.tile_pool(name="opool", bufs=NGROUPS))
+        ps_t = ctx.enter_context(tc.psum_pool(name="ps_t", bufs=5))
+        ps_h = ctx.enter_context(tc.psum_pool(name="ps_h", bufs=2))
+        ps_y = ctx.enter_context(tc.psum_pool(name="ps_y", bufs=1))
+        ctx.enter_context(tc.manual_schedule())
+
+        ident = const.tile([P, P], F32, name="ident")
+        ones = const.tile([P, P], BF16, name="ones")
+        brow = const.tile([P, P], BF16, name="brow")
+        bias4 = const.tile([P, GROUP * P], F32, name="bias4")
+        l_sb = const.tile([P, COLS], BF16, name="l_sb")
+        r_sb = const.tile([P, 512], BF16, name="r_sb")
+        r32 = const.tile([P, 512], F32, name="r32")
+        r_grouped = const.tile([P, 512], BF16, name="r_grouped", align_bytes=64)
+        r_codes = const.tile([P, P], U32, name="r_codes", align_bytes=64)
+        r_scales = const.tile([P, P], U8, name="r_scales", align_bytes=64)
+        l_codes = const.tile([P, 1024], U32, name="l_codes", align_bytes=64)
+        l_scales = const.tile([P, 1024], U8, name="l_scales", align_bytes=64)
+
+        x_tiles = {}
+
+        def load_group(g):
+            x_sb = xpool.tile([P, GROUP * COLS], BF16, name="x_sb")
+            x_tiles[g] = x_sb
+            for t in range(GROUP):
+                nc.sync.dma_start(out=x_sb[:, t * COLS:(t + 1) * COLS], in_=xg[g, :, t, :])
+
+        nc.vector.memset(brow[:], 0.0)
+        nc.vector.memset(ones[:], 1.0)
+        masks.make_identity(nc, ident[:])
+        nc.scalar.dma_start(out=r_sb[:], in_=factorR[0])
+        nc.scalar.dma_start(out=brow[0:1, :], in_=bias.rearrange("(o n) -> o n", o=1))
+        nc.sync.dma_start(
+            out=l_sb[:].rearrange("q (k c) -> q k c", k=KB),
+            in_=factorL.rearrange("k q c -> q k c"),
+        )
+        for g in range(XBUFS):
+            load_group(g)
+
+        def transpose_block(words, grouped, k, engine):
+            bank = ps_t.tile([P, 512], F32, name="bank")
+            for g in range(2):
+                for u in range(2):
+                    src = k * 512 + g * 256 + u * P
+                    dst = u * 256 + g * P
+                    nc.tensor.transpose(bank[:, dst:dst + P], words[:, src:src + P], ident[:])
+            dst_ap = grouped[:].bitcast(F32)[:, k * 512:(k + 1) * 512].rearrange("p (c u) -> p c u", u=2)
+            src_ap = bank[:].rearrange("p (u c) -> p c u", u=2)
+            if engine == "S":
+                nc.scalar.copy(out=dst_ap, in_=src_ap)
+            else:
+                nc.vector.tensor_copy(out=dst_ap, in_=src_ap)
+
+        def quantise(grouped, codes, scales, lo, hi):
+            nc.vector.quantize_mx(
+                out=codes[:, lo:hi].bitcast(FP8X4),
+                scales=scales[:, lo:hi],
+                in_=grouped[:, 4 * lo:4 * hi],
+            )
+
+        bias_ps = ps_t.tile([P, 512], F32, name="bank")
+        nc.tensor.matmul(bias_ps[:, 0:P], lhsT=ones[:], rhs=brow[:], start=True, stop=True)
+        nc.scalar.copy(
+            out=bias4[:].rearrange("p (t s) -> p t s", t=GROUP),
+            in_=bias_ps[:, 0:P].unsqueeze(1).to_broadcast([P, GROUP, P]),
+        )
+
+        nc.vector.tensor_copy(out=r32[:], in_=r_sb[:])
+        r_ps = ps_t.tile([P, 512], F32, name="bank")
+        for t in range(4):
+            nc.tensor.transpose(r_ps[:, t * P:(t + 1) * P], r32[:, t * P:(t + 1) * P], ident[:])
+        nc.vector.tensor_copy(
+            out=r_grouped[:].rearrange("p (s t) -> p s t", t=4),
+            in_=r_ps[:].rearrange("p (t s) -> p s t", t=4),
+        )
+
+        l_grouped = gpool.tile([P, COLS], BF16, name="grouped", align_bytes=64)
+        for k in range(KB):
+            transpose_block(l_sb[:].bitcast(F32), l_grouped, k, "S")
+        quantise(r_grouped, r_codes, r_scales, 0, P)
+        quantise(l_grouped, l_codes, l_scales, 0, 1024)
+
+        grouped_of = {}
+        codes_of = {}
+        h_bank_of = {}
+        h_of = {}
+        y_of = {}
+        o_of = {}
+
+        def stage_t(t):
+            g, j = divmod(t, GROUP)
+            words = x_tiles[g][:].bitcast(F32)[:, j * 2048:(j + 1) * 2048]
+            grouped = gpool.tile([P, COLS], BF16, name="grouped", align_bytes=64)
+            grouped_of[t] = grouped
+            for k in range(KB):
+                transpose_block(words, grouped, k, "S")
+            if j == GROUP - 1 and g + XBUFS < NGROUPS:
+                load_group(g + XBUFS)
+
+        def stage_q(t):
+            codes = cpool.tile([P, 1024], U32, name="codes", align_bytes=64)
+            scales = cpool.tile([P, 1024], U8, name="scales", align_bytes=64)
+            codes_of[t] = (codes, scales)
+            quantise(grouped_of[t], codes, scales, 0, 1024)
+
+        def stage_m(t):
+            codes, scales = codes_of[t]
+            h_bank = ps_h.tile([P, 512], F32, name="h_bank")
+            h_bank_of[t] = h_bank
+            for k in range(KB):
+                for g in range(2):
+                    c = k * 256 + g * P
+                    nc.tensor.matmul_mx(
+                        out=h_bank[:, k * P:(k + 1) * P],
+                        lhsT=l_codes[:, c:c + P].bitcast(FP8X4),
+                        lhsT_scale=l_scales[:, c:c + P],
+                        rhs=codes[:, c:c + P].bitcast(FP8X4),
+                        rhs_scale=scales[:, c:c + P],
+                        start=(g == 0),
+                        stop=(g == 1),
+                    )
+
+        def stage_he(unit, i):
+            if i == 0:
+                h_grouped = hpool.tile([P, UNIT * 512], BF16, name="h_grouped", align_bytes=64)
+                h_codes = hpool.tile([P, UNIT * P], U32, name="h_codes", align_bytes=64)
+                h_scales = hpool.tile([P, UNIT * P], U8, name="h_scales", align_bytes=64)
+                h_of[unit[0]] = (h_grouped, h_codes, h_scales)
+            h_grouped = h_of[unit[0]][0]
+            nc.vector.tensor_copy(
+                out=h_grouped[:, i * 512:(i + 1) * 512].rearrange("p (b k) -> p b k", k=KB),
+                in_=h_bank_of[unit[i]][:].rearrange("p (k b) -> p b k", k=KB),
+            )
+
+        def stage_hq(unit):
+            h_grouped, h_codes, h_scales = h_of[unit[0]]
+            quantise(h_grouped, h_codes, h_scales, 0, UNIT * P)
+
+        def stage_y(unit):
+            h_grouped, h_codes, h_scales = h_of[unit[0]]
+            y_bank = ps_y.tile([P, 512], F32, name="y_bank")
+            y_of[unit[0]] = y_bank
+            for i in range(UNIT):
+                nc.tensor.matmul_mx(
+                    out=y_bank[:, i * P:(i + 1) * P],
+                    lhsT=h_codes[:, i * P:(i + 1) * P].bitcast(FP8X4),
+                    lhsT_scale=h_scales[:, i * P:(i + 1) * P],
+                    rhs=r_codes[:].bitcast(FP8X4),
+                    rhs_scale=r_scales[:],
+                    start=True,
+                    stop=True,
+                )
+
+        pending_stores = []
+
+        def stage_ye(unit):
+            g, j = divmod(unit[0], GROUP)
+            if j == 0:
+                o_of[g] = opool.tile([P, GROUP * P], F32, name="o_sb")
+            o_sb = o_of[g]
+            nc.vector.tensor_tensor(
+                out=o_sb[:, j * P:(j + UNIT) * P],
+                in0=y_of[unit[0]][:, 0:UNIT * P],
+                in1=bias4[:, 0:UNIT * P],
+                op=mybir.AluOpType.add,
+            )
+            if j + UNIT == GROUP:
+                pending_stores.append(g)
+
+        def flush_stores():
+            while pending_stores:
+                g = pending_stores.pop(0)
+                nc.sync.dma_start(out=og[g], in_=o_of[g][:])
+
+        units = [list(range(i, i + UNIT)) for i in range(0, TILES, UNIT)]
+        n_units = len(units)
+        last_load_unit = (NGROUPS - XBUFS) * GROUP // UNIT - 1
+        for n in range(n_units + 2):
+            if n < n_units:
+                for t in units[n]:
+                    stage_t(t)
+            if 0 <= n - 1 < n_units:
+                for t in units[n - 1]:
+                    stage_m(t)
+            if 0 <= n - 2 < n_units:
+                stage_y(units[n - 2])
+            if n < n_units:
+                stage_q(units[n][0])
+            if 0 <= n - 1 < n_units:
+                for i in range(UNIT):
+                    stage_he(units[n - 1], i)
+            if n < n_units:
+                for t in units[n][1:]:
+                    stage_q(t)
+            if 0 <= n - 1 < n_units:
+                stage_hq(units[n - 1])
+            if 0 <= n - 2 < n_units:
+                stage_ye(units[n - 2])
+                if n >= last_load_unit:
+                    flush_stores()

@@ -16,8 +16,9 @@ KB = 4
 TILES = ROWS // P
 GROUP = 4
 NGROUPS = TILES // GROUP
-UNIT = 2
 XBUFS = 4
+M_LAG = 2
+Y_LAG = 4
 
 FLOPS = 2 * ROWS * COLS * 128 + 2 * ROWS * 512 * 128
 
@@ -32,7 +33,7 @@ def tile_butterflyblocksparselinear_t_kernel(tc, x, factorL, factorR, bias, out)
         xpool = ctx.enter_context(tc.tile_pool(name="xpool", bufs=XBUFS))
         gpool = ctx.enter_context(tc.tile_pool(name="gpool", bufs=4))
         cpool = ctx.enter_context(tc.tile_pool(name="cpool", bufs=4))
-        hpool = ctx.enter_context(tc.tile_pool(name="hpool", bufs=3))
+        hpool = ctx.enter_context(tc.tile_pool(name="hpool", bufs=4))
         opool = ctx.enter_context(tc.tile_pool(name="opool", bufs=NGROUPS))
         ps_t = ctx.enter_context(tc.psum_pool(name="ps_t", bufs=5))
         ps_h = ctx.enter_context(tc.psum_pool(name="ps_h", bufs=2))
@@ -42,7 +43,8 @@ def tile_butterflyblocksparselinear_t_kernel(tc, x, factorL, factorR, bias, out)
         ident = const.tile([P, P], F32, name="ident")
         ones = const.tile([P, P], BF16, name="ones")
         brow = const.tile([P, P], BF16, name="brow")
-        bias4 = const.tile([P, GROUP * P], F32, name="bias4")
+        warm = const.tile([P, 1], F32, name="warm")
+        bias_sb = const.tile([P, P], F32, name="bias_sb")
         l_sb = const.tile([P, COLS], BF16, name="l_sb")
         r_sb = const.tile([P, 512], BF16, name="r_sb")
         r32 = const.tile([P, 512], F32, name="r32")
@@ -65,12 +67,17 @@ def tile_butterflyblocksparselinear_t_kernel(tc, x, factorL, factorR, bias, out)
         masks.make_identity(nc, ident[:])
         nc.scalar.dma_start(out=r_sb[:], in_=factorR[0])
         nc.scalar.dma_start(out=brow[0:1, :], in_=bias.rearrange("(o n) -> o n", o=1))
-        nc.sync.dma_start(
-            out=l_sb[:].rearrange("q (k c) -> q k c", k=KB),
-            in_=factorL.rearrange("k q c -> q k c"),
-        )
+        nc.scalar.copy(out=warm[:], in_=ones[:, 0:1])
+        for k in range(KB):
+            nc.sync.dma_start(out=l_sb[:, k * 1024:(k + 1) * 1024], in_=factorL[k])
         for g in range(XBUFS):
             load_group(g)
+
+        def copy_out(engine, dst_ap, src_ap):
+            if engine == "S":
+                nc.scalar.copy(out=dst_ap, in_=src_ap)
+            else:
+                nc.vector.tensor_copy(out=dst_ap, in_=src_ap)
 
         def transpose_block(words, grouped, k, engine):
             bank = ps_t.tile([P, 512], F32, name="bank")
@@ -79,12 +86,11 @@ def tile_butterflyblocksparselinear_t_kernel(tc, x, factorL, factorR, bias, out)
                     src = k * 512 + g * 256 + u * P
                     dst = u * 256 + g * P
                     nc.tensor.transpose(bank[:, dst:dst + P], words[:, src:src + P], ident[:])
-            dst_ap = grouped[:].bitcast(F32)[:, k * 512:(k + 1) * 512].rearrange("p (c u) -> p c u", u=2)
-            src_ap = bank[:].rearrange("p (u c) -> p c u", u=2)
-            if engine == "S":
-                nc.scalar.copy(out=dst_ap, in_=src_ap)
-            else:
-                nc.vector.tensor_copy(out=dst_ap, in_=src_ap)
+            copy_out(
+                engine,
+                grouped[:].bitcast(F32)[:, k * 512:(k + 1) * 512].rearrange("p (c u) -> p c u", u=2),
+                bank[:].rearrange("p (u c) -> p c u", u=2),
+            )
 
         def quantise(grouped, codes, scales, lo, hi):
             nc.vector.quantize_mx(
@@ -92,28 +98,6 @@ def tile_butterflyblocksparselinear_t_kernel(tc, x, factorL, factorR, bias, out)
                 scales=scales[:, lo:hi],
                 in_=grouped[:, 4 * lo:4 * hi],
             )
-
-        bias_ps = ps_t.tile([P, 512], F32, name="bank")
-        nc.tensor.matmul(bias_ps[:, 0:P], lhsT=ones[:], rhs=brow[:], start=True, stop=True)
-        nc.scalar.copy(
-            out=bias4[:].rearrange("p (t s) -> p t s", t=GROUP),
-            in_=bias_ps[:, 0:P].unsqueeze(1).to_broadcast([P, GROUP, P]),
-        )
-
-        nc.vector.tensor_copy(out=r32[:], in_=r_sb[:])
-        r_ps = ps_t.tile([P, 512], F32, name="bank")
-        for t in range(4):
-            nc.tensor.transpose(r_ps[:, t * P:(t + 1) * P], r32[:, t * P:(t + 1) * P], ident[:])
-        nc.vector.tensor_copy(
-            out=r_grouped[:].rearrange("p (s t) -> p s t", t=4),
-            in_=r_ps[:].rearrange("p (t s) -> p s t", t=4),
-        )
-
-        l_grouped = gpool.tile([P, COLS], BF16, name="grouped", align_bytes=64)
-        for k in range(KB):
-            transpose_block(l_sb[:].bitcast(F32), l_grouped, k, "S")
-        quantise(r_grouped, r_codes, r_scales, 0, P)
-        quantise(l_grouped, l_codes, l_scales, 0, 1024)
 
         grouped_of = {}
         codes_of = {}
@@ -132,17 +116,20 @@ def tile_butterflyblocksparselinear_t_kernel(tc, x, factorL, factorR, bias, out)
             if j == GROUP - 1 and g + XBUFS < NGROUPS:
                 load_group(g + XBUFS)
 
-        def stage_q(t):
-            codes = cpool.tile([P, 1024], U32, name="codes", align_bytes=64)
-            scales = cpool.tile([P, 1024], U8, name="scales", align_bytes=64)
-            codes_of[t] = (codes, scales)
-            quantise(grouped_of[t], codes, scales, 0, 1024)
-
-        def stage_m(t):
+        def stage_q(t, k0=0, k1=KB):
+            if k0 == 0:
+                codes = cpool.tile([P, 1024], U32, name="codes", align_bytes=64)
+                scales = cpool.tile([P, 1024], U8, name="scales", align_bytes=64)
+                codes_of[t] = (codes, scales)
             codes, scales = codes_of[t]
-            h_bank = ps_h.tile([P, 512], F32, name="h_bank")
-            h_bank_of[t] = h_bank
-            for k in range(KB):
+            quantise(grouped_of[t], codes, scales, k0 * 256, k1 * 256)
+
+        def stage_m(t, k0=0, k1=KB):
+            codes, scales = codes_of[t]
+            if k0 == 0:
+                h_bank_of[t] = ps_h.tile([P, 512], F32, name="h_bank")
+            h_bank = h_bank_of[t]
+            for k in range(k0, k1):
                 for g in range(2):
                     c = k * 256 + g * P
                     nc.tensor.matmul_mx(
@@ -155,81 +142,131 @@ def tile_butterflyblocksparselinear_t_kernel(tc, x, factorL, factorR, bias, out)
                         stop=(g == 1),
                     )
 
-        def stage_he(unit, i):
-            if i == 0:
-                h_grouped = hpool.tile([P, UNIT * 512], BF16, name="h_grouped", align_bytes=64)
-                h_codes = hpool.tile([P, UNIT * P], U32, name="h_codes", align_bytes=64)
-                h_scales = hpool.tile([P, UNIT * P], U8, name="h_scales", align_bytes=64)
-                h_of[unit[0]] = (h_grouped, h_codes, h_scales)
-            h_grouped = h_of[unit[0]][0]
-            nc.vector.tensor_copy(
-                out=h_grouped[:, i * 512:(i + 1) * 512].rearrange("p (b k) -> p b k", k=KB),
-                in_=h_bank_of[unit[i]][:].rearrange("p (k b) -> p b k", k=KB),
+        def stage_he(t, engine):
+            h_grouped = hpool.tile([P, 512], BF16, name="h_grouped", align_bytes=64)
+            h_codes = hpool.tile([P, P], U32, name="h_codes", align_bytes=64)
+            h_scales = hpool.tile([P, P], U8, name="h_scales", align_bytes=64)
+            h_of[t] = (h_grouped, h_codes, h_scales)
+            copy_out(
+                engine,
+                h_grouped[:].rearrange("p (b k) -> p b k", k=KB),
+                h_bank_of[t][:].rearrange("p (k b) -> p b k", k=KB),
             )
 
-        def stage_hq(unit):
-            h_grouped, h_codes, h_scales = h_of[unit[0]]
-            quantise(h_grouped, h_codes, h_scales, 0, UNIT * P)
+        def stage_hq(t):
+            h_grouped, h_codes, h_scales = h_of[t]
+            quantise(h_grouped, h_codes, h_scales, 0, P)
 
-        def stage_y(unit):
-            h_grouped, h_codes, h_scales = h_of[unit[0]]
-            y_bank = ps_y.tile([P, 512], F32, name="y_bank")
-            y_of[unit[0]] = y_bank
-            for i in range(UNIT):
-                nc.tensor.matmul_mx(
-                    out=y_bank[:, i * P:(i + 1) * P],
-                    lhsT=h_codes[:, i * P:(i + 1) * P].bitcast(FP8X4),
-                    lhsT_scale=h_scales[:, i * P:(i + 1) * P],
-                    rhs=r_codes[:].bitcast(FP8X4),
-                    rhs_scale=r_scales[:],
-                    start=True,
-                    stop=True,
-                )
+        def stage_y(t, pool):
+            h_grouped, h_codes, h_scales = h_of[t]
+            if pool == "y":
+                y_bank = ps_y.tile([P, 512], F32, name="y_bank")
+            else:
+                y_bank = ps_t.tile([P, 512], F32, name="bank")
+            y_of[t] = y_bank
+            nc.tensor.matmul_mx(
+                out=y_bank[:, 0:P],
+                lhsT=h_codes[:].bitcast(FP8X4),
+                lhsT_scale=h_scales[:],
+                rhs=r_codes[:].bitcast(FP8X4),
+                rhs_scale=r_scales[:],
+                start=True,
+                stop=True,
+            )
 
-        pending_stores = []
-
-        def stage_ye(unit):
-            g, j = divmod(unit[0], GROUP)
+        def stage_ye(t):
+            g, j = divmod(t, GROUP)
             if j == 0:
                 o_of[g] = opool.tile([P, GROUP * P], F32, name="o_sb")
-            o_sb = o_of[g]
             nc.vector.tensor_tensor(
-                out=o_sb[:, j * P:(j + UNIT) * P],
-                in0=y_of[unit[0]][:, 0:UNIT * P],
-                in1=bias4[:, 0:UNIT * P],
+                out=o_of[g][:, j * P:(j + 1) * P],
+                in0=y_of[t][:, 0:P],
+                in1=bias_sb[:],
                 op=mybir.AluOpType.add,
             )
-            if j + UNIT == GROUP:
-                pending_stores.append(g)
 
-        def flush_stores():
-            while pending_stores:
-                g = pending_stores.pop(0)
-                nc.sync.dma_start(out=og[g], in_=o_of[g][:])
+        def store(g, j0, j1):
+            nc.sync.dma_start(out=og[g][:, j0 * P:j1 * P], in_=o_of[g][:, j0 * P:j1 * P])
 
-        units = [list(range(i, i + UNIT)) for i in range(0, TILES, UNIT)]
-        n_units = len(units)
-        last_load_unit = (NGROUPS - XBUFS) * GROUP // UNIT - 1
-        for n in range(n_units + 2):
-            if n < n_units:
-                for t in units[n]:
-                    stage_t(t)
-            if 0 <= n - 1 < n_units:
-                for t in units[n - 1]:
-                    stage_m(t)
-            if 0 <= n - 2 < n_units:
-                stage_y(units[n - 2])
-            if n < n_units:
-                stage_q(units[n][0])
-            if 0 <= n - 1 < n_units:
-                for i in range(UNIT):
-                    stage_he(units[n - 1], i)
-            if n < n_units:
-                for t in units[n][1:]:
-                    stage_q(t)
-            if 0 <= n - 1 < n_units:
-                stage_hq(units[n - 1])
-            if 0 <= n - 2 < n_units:
-                stage_ye(units[n - 2])
-                if n >= last_load_unit:
-                    flush_stores()
+        def small_operands_front():
+            nc.vector.tensor_copy(out=r32[:], in_=r_sb[:])
+            bias_ps = ps_t.tile([P, 512], F32, name="bank")
+            nc.tensor.matmul(bias_ps[:, 0:P], lhsT=ones[:], rhs=brow[:], start=True, stop=True)
+            nc.scalar.copy(out=bias_sb[:], in_=bias_ps[:, 0:P])
+            r_ps = ps_t.tile([P, 512], F32, name="bank")
+            for t in range(4):
+                nc.tensor.transpose(r_ps[:, t * P:(t + 1) * P], r32[:, t * P:(t + 1) * P], ident[:])
+            nc.vector.tensor_copy(
+                out=r_grouped[:].rearrange("p (s t) -> p s t", t=4),
+                in_=r_ps[:].rearrange("p (t s) -> p s t", t=4),
+            )
+
+        l_grouped = gpool.tile([P, COLS], BF16, name="grouped", align_bytes=64)
+        for k in range(KB):
+            transpose_block(l_sb[:].bitcast(F32), l_grouped, k, "S")
+        quantise(l_grouped, l_codes, l_scales, 0, 1024)
+
+        last = TILES - 1
+        last_load_tile = (NGROUPS - XBUFS) * GROUP - 1
+        ready_groups = []
+        for i in range(last - 1):
+            stage_t(i)
+            if i == 1:
+                small_operands_front()
+            if i >= M_LAG:
+                stage_m(i - M_LAG)
+            if i >= Y_LAG:
+                stage_y(i - Y_LAG, "y")
+            if i >= M_LAG:
+                stage_he(i - M_LAG, "V")
+            if i >= Y_LAG:
+                stage_ye(i - Y_LAG)
+                if (i - Y_LAG) % GROUP == GROUP - 1:
+                    ready_groups.append((i - Y_LAG) // GROUP)
+                if i >= last_load_tile:
+                    for g in ready_groups:
+                        store(g, 0, GROUP)
+                    ready_groups = []
+            stage_q(i)
+            if i == 1:
+                quantise(r_grouped, r_codes, r_scales, 0, P)
+            if i >= M_LAG:
+                stage_hq(i - M_LAG)
+
+        i = last - 1
+        stage_t(i)
+        stage_m(i - 2)
+        stage_y(i - 4, "y")
+        stage_q(i, 0, 2)
+        stage_he(i - 2, "V")
+        stage_q(i, 2, 4)
+        stage_ye(i - 4)
+        stage_hq(i - 2)
+
+        i = last
+        stage_t(i)
+        stage_m(i - 2)
+        stage_y(i - 4, "y")
+        stage_q(i, 0, 2)
+        stage_ye(i - 4)
+        store((i - 4) // GROUP, 0, GROUP)
+        stage_he(i - 2, "S")
+        stage_q(i, 2, 4)
+        stage_m(i - 1)
+        stage_he(i - 1, "S")
+        stage_m(i, 0, 2)
+        stage_m(i, 2, 4)
+        stage_he(i, "S")
+        stage_hq(i - 2)
+        stage_y(i - 3, "t")
+        stage_ye(i - 3)
+        stage_hq(i - 1)
+        stage_y(i - 2, "t")
+        stage_ye(i - 2)
+        stage_hq(i)
+        stage_y(i - 1, "t")
+        stage_ye(i - 1)
+        store(NGROUPS - 1, 0, GROUP - 1)
+        stage_y(i, "t")
+        stage_ye(i)
+        store(NGROUPS - 1, GROUP - 1, GROUP)

@@ -33,7 +33,7 @@ def tile_butterflyblocksparselinear_t_kernel(tc, x, factorL, factorR, bias, out)
         xpool = ctx.enter_context(tc.tile_pool(name="xpool", bufs=XBUFS))
         gpool = ctx.enter_context(tc.tile_pool(name="gpool", bufs=4))
         cpool = ctx.enter_context(tc.tile_pool(name="cpool", bufs=4))
-        hpool = ctx.enter_context(tc.tile_pool(name="hpool", bufs=4))
+        hpool = ctx.enter_context(tc.tile_pool(name="hpool", bufs=6))
         opool = ctx.enter_context(tc.tile_pool(name="opool", bufs=NGROUPS))
         ps_t = ctx.enter_context(tc.psum_pool(name="ps_t", bufs=5))
         ps_h = ctx.enter_context(tc.psum_pool(name="ps_h", bufs=2))
@@ -41,7 +41,7 @@ def tile_butterflyblocksparselinear_t_kernel(tc, x, factorL, factorR, bias, out)
         ctx.enter_context(tc.manual_schedule())
 
         ident = const.tile([P, P], F32, name="ident")
-        ones = const.tile([P, P], BF16, name="ones")
+        wide = const.tile([P, 512], BF16, name="wide")
         brow = const.tile([P, P], BF16, name="brow")
         warm = const.tile([P, 1], F32, name="warm")
         bias_sb = const.tile([P, P], F32, name="bias_sb")
@@ -62,16 +62,24 @@ def tile_butterflyblocksparselinear_t_kernel(tc, x, factorL, factorR, bias, out)
             for t in range(GROUP):
                 nc.sync.dma_start(out=x_sb[:, t * COLS:(t + 1) * COLS], in_=xg[g, :, t, :])
 
+        nc.vector.memset(wide[:], 1.0)
         nc.vector.memset(brow[:], 0.0)
-        nc.vector.memset(ones[:], 1.0)
         masks.make_identity(nc, ident[:])
         nc.scalar.dma_start(out=r_sb[:], in_=factorR[0])
         nc.scalar.dma_start(out=brow[0:1, :], in_=bias.rearrange("(o n) -> o n", o=1))
-        nc.scalar.copy(out=warm[:], in_=ones[:, 0:1])
+        nc.scalar.copy(out=warm[:], in_=wide[:, 0:1])
         for k in range(KB):
             nc.sync.dma_start(out=l_sb[:, k * 1024:(k + 1) * 1024], in_=factorL[k])
         for g in range(XBUFS):
             load_group(g)
+
+        warm_ps = ps_h.tile([P, 512], F32, name="h_bank")
+
+        def warm_up(n):
+            for r in range(n):
+                nc.tensor.matmul(warm_ps[:], lhsT=wide[:, 0:P], rhs=wide[:], start=True, stop=True)
+
+        warm_up(7)
 
         def copy_out(engine, dst_ap, src_ap):
             if engine == "S":
@@ -124,10 +132,12 @@ def tile_butterflyblocksparselinear_t_kernel(tc, x, factorL, factorR, bias, out)
             codes, scales = codes_of[t]
             quantise(grouped_of[t], codes, scales, k0 * 256, k1 * 256)
 
-        def stage_m(t, k0=0, k1=KB):
+        def stage_m(t, k0=0, k1=KB, pool="h"):
             codes, scales = codes_of[t]
-            if k0 == 0:
+            if k0 == 0 and pool == "h":
                 h_bank_of[t] = ps_h.tile([P, 512], F32, name="h_bank")
+            if k0 == 0 and pool == "t":
+                h_bank_of[t] = ps_t.tile([P, 512], F32, name="bank")
             h_bank = h_bank_of[t]
             for k in range(k0, k1):
                 for g in range(2):
@@ -191,7 +201,7 @@ def tile_butterflyblocksparselinear_t_kernel(tc, x, factorL, factorR, bias, out)
         def small_operands_front():
             nc.vector.tensor_copy(out=r32[:], in_=r_sb[:])
             bias_ps = ps_t.tile([P, 512], F32, name="bank")
-            nc.tensor.matmul(bias_ps[:, 0:P], lhsT=ones[:], rhs=brow[:], start=True, stop=True)
+            nc.tensor.matmul(bias_ps[:, 0:P], lhsT=wide[:, 0:P], rhs=brow[:], start=True, stop=True)
             nc.scalar.copy(out=bias_sb[:], in_=bias_ps[:, 0:P])
             r_ps = ps_t.tile([P, 512], F32, name="bank")
             for t in range(4):
@@ -204,6 +214,7 @@ def tile_butterflyblocksparselinear_t_kernel(tc, x, factorL, factorR, bias, out)
         l_grouped = gpool.tile([P, COLS], BF16, name="grouped", align_bytes=64)
         for k in range(KB):
             transpose_block(l_sb[:].bitcast(F32), l_grouped, k, "S")
+        warm_up(3)
         quantise(l_grouped, l_codes, l_scales, 0, 1024)
 
         last = TILES - 1
@@ -211,8 +222,11 @@ def tile_butterflyblocksparselinear_t_kernel(tc, x, factorL, factorR, bias, out)
         ready_groups = []
         for i in range(last - 1):
             stage_t(i)
+            if i == 0:
+                warm_up(3)
             if i == 1:
                 small_operands_front()
+                warm_up(2)
             if i >= M_LAG:
                 stage_m(i - M_LAG)
             if i >= Y_LAG:
@@ -240,33 +254,35 @@ def tile_butterflyblocksparselinear_t_kernel(tc, x, factorL, factorR, bias, out)
         stage_q(i, 0, 2)
         stage_he(i - 2, "V")
         stage_q(i, 2, 4)
-        stage_ye(i - 4)
-        stage_hq(i - 2)
 
         i = last
         stage_t(i)
         stage_m(i - 2)
-        stage_y(i - 4, "y")
-        stage_q(i, 0, 2)
-        stage_ye(i - 4)
-        store((i - 4) // GROUP, 0, GROUP)
         stage_he(i - 2, "S")
-        stage_q(i, 2, 4)
+        stage_q(i, 0, 2)
         stage_m(i - 1)
         stage_he(i - 1, "S")
-        stage_m(i, 0, 2)
-        stage_m(i, 2, 4)
+        stage_q(i, 2, 3)
+        stage_q(i, 3, 4)
+        stage_m(i, 0, 2, "t")
+        stage_m(i, 2, 3, "t")
+        stage_m(i, 3, 4, "t")
         stage_he(i, "S")
+        stage_ye(i - 5)
+        stage_hq(i - 3)
         stage_hq(i - 2)
+        stage_hq(i - 1)
+        stage_y(i - 4, "t")
+        stage_ye(i - 4)
+        store((i - 4) // GROUP, 0, GROUP)
         stage_y(i - 3, "t")
         stage_ye(i - 3)
-        stage_hq(i - 1)
+        stage_hq(i)
         stage_y(i - 2, "t")
         stage_ye(i - 2)
-        stage_hq(i)
+        store(NGROUPS - 1, 0, 2)
         stage_y(i - 1, "t")
         stage_ye(i - 1)
-        store(NGROUPS - 1, 0, GROUP - 1)
         stage_y(i, "t")
         stage_ye(i)
-        store(NGROUPS - 1, GROUP - 1, GROUP)
+        store(NGROUPS - 1, 2, GROUP)

@@ -18,7 +18,8 @@ GROUP = 4
 NGROUPS = TILES // GROUP
 XBUFS = 4
 M_LAG = 2
-Y_LAG = 4
+Y_LAG = 2
+V_SHARE = 2
 
 FLOPS = 2 * ROWS * COLS * 128 + 2 * ROWS * 512 * 128
 
@@ -33,7 +34,7 @@ def tile_butterflyblocksparselinear_t_kernel(tc, x, factorL, factorR, bias, out)
         xpool = ctx.enter_context(tc.tile_pool(name="xpool", bufs=XBUFS))
         gpool = ctx.enter_context(tc.tile_pool(name="gpool", bufs=4))
         cpool = ctx.enter_context(tc.tile_pool(name="cpool", bufs=4))
-        hpool = ctx.enter_context(tc.tile_pool(name="hpool", bufs=6))
+        hpool = ctx.enter_context(tc.tile_pool(name="hpool", bufs=2))
         opool = ctx.enter_context(tc.tile_pool(name="opool", bufs=NGROUPS))
         ps_t = ctx.enter_context(tc.psum_pool(name="ps_t", bufs=5))
         ps_h = ctx.enter_context(tc.psum_pool(name="ps_h", bufs=2))
@@ -41,10 +42,10 @@ def tile_butterflyblocksparselinear_t_kernel(tc, x, factorL, factorR, bias, out)
         ctx.enter_context(tc.manual_schedule())
 
         ident = const.tile([P, P], F32, name="ident")
-        wide = const.tile([P, 512], BF16, name="wide")
+        ones = const.tile([P, P], BF16, name="ones")
         brow = const.tile([P, P], BF16, name="brow")
         warm = const.tile([P, 1], F32, name="warm")
-        bias_sb = const.tile([P, P], F32, name="bias_sb")
+        bias4 = const.tile([P, GROUP * P], F32, name="bias4")
         l_sb = const.tile([P, COLS], BF16, name="l_sb")
         r_sb = const.tile([P, 512], BF16, name="r_sb")
         r32 = const.tile([P, 512], F32, name="r32")
@@ -62,24 +63,16 @@ def tile_butterflyblocksparselinear_t_kernel(tc, x, factorL, factorR, bias, out)
             for t in range(GROUP):
                 nc.sync.dma_start(out=x_sb[:, t * COLS:(t + 1) * COLS], in_=xg[g, :, t, :])
 
-        nc.vector.memset(wide[:], 1.0)
         nc.vector.memset(brow[:], 0.0)
+        nc.vector.memset(ones[:], 1.0)
         masks.make_identity(nc, ident[:])
         nc.scalar.dma_start(out=r_sb[:], in_=factorR[0])
         nc.scalar.dma_start(out=brow[0:1, :], in_=bias.rearrange("(o n) -> o n", o=1))
-        nc.scalar.copy(out=warm[:], in_=wide[:, 0:1])
+        nc.scalar.copy(out=warm[:], in_=ones[:, 0:1])
         for k in range(KB):
             nc.sync.dma_start(out=l_sb[:, k * 1024:(k + 1) * 1024], in_=factorL[k])
         for g in range(XBUFS):
             load_group(g)
-
-        warm_ps = ps_h.tile([P, 512], F32, name="h_bank")
-
-        def warm_up(n):
-            for r in range(n):
-                nc.tensor.matmul(warm_ps[:], lhsT=wide[:, 0:P], rhs=wide[:], start=True, stop=True)
-
-        warm_up(7)
 
         def copy_out(engine, dst_ap, src_ap):
             if engine == "S":
@@ -114,13 +107,13 @@ def tile_butterflyblocksparselinear_t_kernel(tc, x, factorL, factorR, bias, out)
         y_of = {}
         o_of = {}
 
-        def stage_t(t):
+        def stage_t(t, last_engine="S"):
             g, j = divmod(t, GROUP)
             words = x_tiles[g][:].bitcast(F32)[:, j * 2048:(j + 1) * 2048]
             grouped = gpool.tile([P, COLS], BF16, name="grouped", align_bytes=64)
             grouped_of[t] = grouped
             for k in range(KB):
-                transpose_block(words, grouped, k, "S")
+                transpose_block(words, grouped, k, last_engine if k == KB - 1 else "S")
             if j == GROUP - 1 and g + XBUFS < NGROUPS:
                 load_group(g + XBUFS)
 
@@ -153,45 +146,51 @@ def tile_butterflyblocksparselinear_t_kernel(tc, x, factorL, factorR, bias, out)
                     )
 
         def stage_he(t, engine):
-            h_grouped = hpool.tile([P, 512], BF16, name="h_grouped", align_bytes=64)
-            h_codes = hpool.tile([P, P], U32, name="h_codes", align_bytes=64)
-            h_scales = hpool.tile([P, P], U8, name="h_scales", align_bytes=64)
-            h_of[t] = (h_grouped, h_codes, h_scales)
+            g, j = divmod(t, GROUP)
+            if j == 0:
+                h_grouped = hpool.tile([P, GROUP * 512], BF16, name="h_grouped", align_bytes=64)
+                h_codes = hpool.tile([P, GROUP * P], U32, name="h_codes", align_bytes=64)
+                h_scales = hpool.tile([P, GROUP * P], U8, name="h_scales", align_bytes=64)
+                h_of[g] = (h_grouped, h_codes, h_scales)
             copy_out(
                 engine,
-                h_grouped[:].rearrange("p (b k) -> p b k", k=KB),
+                h_of[g][0][:, j * 512:(j + 1) * 512].rearrange("p (b k) -> p b k", k=KB),
                 h_bank_of[t][:].rearrange("p (k b) -> p b k", k=KB),
             )
 
-        def stage_hq(t):
-            h_grouped, h_codes, h_scales = h_of[t]
-            quantise(h_grouped, h_codes, h_scales, 0, P)
+        def stage_hq(t, n):
+            g, j = divmod(t, GROUP)
+            h_grouped, h_codes, h_scales = h_of[g]
+            quantise(h_grouped, h_codes, h_scales, j * P, (j + n) * P)
 
-        def stage_y(t, pool):
-            h_grouped, h_codes, h_scales = h_of[t]
+        def stage_y(t, n, pool):
+            g, j = divmod(t, GROUP)
+            h_grouped, h_codes, h_scales = h_of[g]
             if pool == "y":
                 y_bank = ps_y.tile([P, 512], F32, name="y_bank")
             else:
                 y_bank = ps_t.tile([P, 512], F32, name="bank")
             y_of[t] = y_bank
-            nc.tensor.matmul_mx(
-                out=y_bank[:, 0:P],
-                lhsT=h_codes[:].bitcast(FP8X4),
-                lhsT_scale=h_scales[:],
-                rhs=r_codes[:].bitcast(FP8X4),
-                rhs_scale=r_scales[:],
-                start=True,
-                stop=True,
-            )
+            for r in range(n):
+                c = (j + r) * P
+                nc.tensor.matmul_mx(
+                    out=y_bank[:, r * P:(r + 1) * P],
+                    lhsT=h_codes[:, c:c + P].bitcast(FP8X4),
+                    lhsT_scale=h_scales[:, c:c + P],
+                    rhs=r_codes[:].bitcast(FP8X4),
+                    rhs_scale=r_scales[:],
+                    start=True,
+                    stop=True,
+                )
 
-        def stage_ye(t):
+        def stage_ye(t, n):
             g, j = divmod(t, GROUP)
             if j == 0:
                 o_of[g] = opool.tile([P, GROUP * P], F32, name="o_sb")
             nc.vector.tensor_tensor(
-                out=o_of[g][:, j * P:(j + 1) * P],
-                in0=y_of[t][:, 0:P],
-                in1=bias_sb[:],
+                out=o_of[g][:, j * P:(j + n) * P],
+                in0=y_of[t][:, 0:n * P],
+                in1=bias4[:, 0:n * P],
                 op=mybir.AluOpType.add,
             )
 
@@ -201,8 +200,11 @@ def tile_butterflyblocksparselinear_t_kernel(tc, x, factorL, factorR, bias, out)
         def small_operands_front():
             nc.vector.tensor_copy(out=r32[:], in_=r_sb[:])
             bias_ps = ps_t.tile([P, 512], F32, name="bank")
-            nc.tensor.matmul(bias_ps[:, 0:P], lhsT=wide[:, 0:P], rhs=brow[:], start=True, stop=True)
-            nc.scalar.copy(out=bias_sb[:], in_=bias_ps[:, 0:P])
+            nc.tensor.matmul(bias_ps[:, 0:P], lhsT=ones[:], rhs=brow[:], start=True, stop=True)
+            nc.scalar.copy(
+                out=bias4[:].rearrange("p (t s) -> p t s", t=GROUP),
+                in_=bias_ps[:, 0:P].unsqueeze(1).to_broadcast([P, GROUP, P]),
+            )
             r_ps = ps_t.tile([P, 512], F32, name="bank")
             for t in range(4):
                 nc.tensor.transpose(r_ps[:, t * P:(t + 1) * P], r32[:, t * P:(t + 1) * P], ident[:])
@@ -214,43 +216,41 @@ def tile_butterflyblocksparselinear_t_kernel(tc, x, factorL, factorR, bias, out)
         l_grouped = gpool.tile([P, COLS], BF16, name="grouped", align_bytes=64)
         for k in range(KB):
             transpose_block(l_sb[:].bitcast(F32), l_grouped, k, "S")
-        warm_up(3)
         quantise(l_grouped, l_codes, l_scales, 0, 1024)
 
         last = TILES - 1
         last_load_tile = (NGROUPS - XBUFS) * GROUP - 1
         ready_groups = []
         for i in range(last - 1):
-            stage_t(i)
-            if i == 0:
-                warm_up(3)
+            hq_group, hq_rest = divmod(i - M_LAG - (GROUP - 1), GROUP)
+            y_group, y_rest = divmod(i - M_LAG - Y_LAG - (GROUP - 1), GROUP)
+            do_hq = hq_rest == 0 and hq_group >= 0
+            do_y = y_rest == 0 and y_group >= 0
+            stage_t(i, "V" if (i % GROUP == V_SHARE and i < last - GROUP) else "S")
             if i == 1:
                 small_operands_front()
-                warm_up(2)
             if i >= M_LAG:
                 stage_m(i - M_LAG)
-            if i >= Y_LAG:
-                stage_y(i - Y_LAG, "y")
+            if do_y:
+                stage_y(y_group * GROUP, GROUP, "y")
             if i >= M_LAG:
                 stage_he(i - M_LAG, "V")
-            if i >= Y_LAG:
-                stage_ye(i - Y_LAG)
-                if (i - Y_LAG) % GROUP == GROUP - 1:
-                    ready_groups.append((i - Y_LAG) // GROUP)
-                if i >= last_load_tile:
-                    for g in ready_groups:
-                        store(g, 0, GROUP)
-                    ready_groups = []
+            if do_y:
+                stage_ye(y_group * GROUP, GROUP)
+                ready_groups.append(y_group)
+            if i >= last_load_tile:
+                for g in ready_groups:
+                    store(g, 0, GROUP)
+                ready_groups = []
             stage_q(i)
             if i == 1:
                 quantise(r_grouped, r_codes, r_scales, 0, P)
-            if i >= M_LAG:
-                stage_hq(i - M_LAG)
+            if do_hq:
+                stage_hq(hq_group * GROUP, GROUP)
 
         i = last - 1
         stage_t(i)
         stage_m(i - 2)
-        stage_y(i - 4, "y")
         stage_q(i, 0, 2)
         stage_he(i - 2, "V")
         stage_q(i, 2, 4)
@@ -258,6 +258,7 @@ def tile_butterflyblocksparselinear_t_kernel(tc, x, factorL, factorR, bias, out)
         i = last
         stage_t(i)
         stage_m(i - 2)
+        stage_y(i - 7, GROUP, "y")
         stage_he(i - 2, "S")
         stage_q(i, 0, 2)
         stage_m(i - 1)
@@ -268,21 +269,14 @@ def tile_butterflyblocksparselinear_t_kernel(tc, x, factorL, factorR, bias, out)
         stage_m(i, 2, 3, "t")
         stage_m(i, 3, 4, "t")
         stage_he(i, "S")
-        stage_ye(i - 5)
-        stage_hq(i - 3)
-        stage_hq(i - 2)
-        stage_hq(i - 1)
-        stage_y(i - 4, "t")
-        stage_ye(i - 4)
-        store((i - 4) // GROUP, 0, GROUP)
-        stage_y(i - 3, "t")
-        stage_ye(i - 3)
-        stage_hq(i)
-        stage_y(i - 2, "t")
-        stage_ye(i - 2)
+        stage_ye(i - 7, GROUP)
+        store(NGROUPS - 2, 0, GROUP)
+        stage_hq(i - 3, 2)
+        stage_hq(i - 1, 1)
+        stage_y(i - 3, 2, "t")
+        stage_hq(i, 1)
+        stage_ye(i - 3, 2)
         store(NGROUPS - 1, 0, 2)
-        stage_y(i - 1, "t")
-        stage_ye(i - 1)
-        stage_y(i, "t")
-        stage_ye(i)
+        stage_y(i - 1, 2, "t")
+        stage_ye(i - 1, 2)
         store(NGROUPS - 1, 2, GROUP)

@@ -80,8 +80,13 @@ def tile_butterflyblocksparselinear_t_kernel(tc, x, factorL, factorR, bias, out)
             else:
                 nc.vector.tensor_copy(out=dst_ap, in_=src_ap)
 
-        def transpose_block(words, grouped, k, engine):
+        def bridge(bank):
+            nc.tensor.matmul(bank[:, 0:32], lhsT=ones[:], rhs=ones[:, 0:32], start=True, stop=True)
+
+        def transpose_block(words, grouped, k, engine, bridged=False):
             bank = ps_t.tile([P, 512], F32, name="bank")
+            if bridged:
+                bridge(bank)
             for g in range(2):
                 for u in range(2):
                     src = k * 512 + g * 256 + u * P
@@ -113,7 +118,7 @@ def tile_butterflyblocksparselinear_t_kernel(tc, x, factorL, factorR, bias, out)
             grouped = gpool.tile([P, COLS], BF16, name="grouped", align_bytes=64)
             grouped_of[t] = grouped
             for k in range(KB):
-                transpose_block(words, grouped, k, last_engine if k == KB - 1 else "S")
+                transpose_block(words, grouped, k, last_engine if k == KB - 1 else "S", k == 0 and t > M_LAG)
             if j == GROUP - 1 and g + XBUFS < NGROUPS:
                 load_group(g + XBUFS)
 
@@ -125,13 +130,15 @@ def tile_butterflyblocksparselinear_t_kernel(tc, x, factorL, factorR, bias, out)
             codes, scales = codes_of[t]
             quantise(grouped_of[t], codes, scales, k0 * 256, k1 * 256)
 
-        def stage_m(t, k0=0, k1=KB, pool="h"):
+        def stage_m(t, k0=0, k1=KB, pool="h", bridged=False):
             codes, scales = codes_of[t]
             if k0 == 0 and pool == "h":
                 h_bank_of[t] = ps_h.tile([P, 512], F32, name="h_bank")
             if k0 == 0 and pool == "t":
                 h_bank_of[t] = ps_t.tile([P, 512], F32, name="bank")
             h_bank = h_bank_of[t]
+            if bridged:
+                bridge(h_bank)
             for k in range(k0, k1):
                 for g in range(2):
                     c = k * 256 + g * P
@@ -230,7 +237,7 @@ def tile_butterflyblocksparselinear_t_kernel(tc, x, factorL, factorR, bias, out)
             if i == 1:
                 small_operands_front()
             if i >= M_LAG:
-                stage_m(i - M_LAG)
+                stage_m(i - M_LAG, bridged=True)
             if do_y:
                 stage_y(y_group * GROUP, GROUP, "y")
             if i >= M_LAG:
@@ -250,14 +257,14 @@ def tile_butterflyblocksparselinear_t_kernel(tc, x, factorL, factorR, bias, out)
 
         i = last - 1
         stage_t(i)
-        stage_m(i - 2)
+        stage_m(i - 2, bridged=True)
         stage_q(i, 0, 2)
         stage_he(i - 2, "V")
         stage_q(i, 2, 4)
 
         i = last
         stage_t(i)
-        stage_m(i - 2)
+        stage_m(i - 2, bridged=True)
         stage_y(i - 7, GROUP, "y")
         stage_he(i - 2, "S")
         stage_q(i, 0, 2)

from contextlib import ExitStack

import concourse.masks as masks
import concourse.mybir as mybir

FP8X4 = mybir.dt.float8_e4m3fn_x4
BF16 = mybir.dt.bfloat16
F32 = mybir.dt.float32
U32 = mybir.dt.uint32
U8 = mybir.dt.uint8

P = 128
ROWS = 4096
COLS = 4096
KB = 4
TILES = ROWS // P
GROUP = 4
NGROUPS = TILES // GROUP
XBUFS = 4
M_LAG = 2
Y_LAG = 2
V_SHARE = 2

FLOPS = 2 * ROWS * COLS * 128 + 2 * ROWS * 512 * 128


def tile_butterflyblocksparselinear_t_kernel(tc, x, factorL, factorR, bias, out):
    nc = tc.nc
    xg = x.flatten_outer_dims().rearrange("(g p t) c -> g p t c", p=P, t=GROUP)
    og = out.flatten_outer_dims().rearrange("(g p t) s -> g p (t s)", p=P, t=GROUP)

    with ExitStack() as ctx:
        const = ctx.enter_context(tc.tile_pool(name="const", bufs=1))
        xpool = ctx.enter_context(tc.tile_pool(name="xpool", bufs=XBUFS))
        gpool = ctx.enter_context(tc.tile_pool(name="gpool", bufs=4))
        cpool = ctx.enter_context(tc.tile_pool(name="cpool", bufs=4))
        hpool = ctx.enter_context(tc.tile_pool(name="hpool", bufs=2))
        opool = ctx.enter_context(tc.tile_pool(name="opool", bufs=NGROUPS))
        ps_t = ctx.enter_context(tc.psum_pool(name="ps_t", bufs=5))
        ps_h = ctx.enter_context(tc.psum_pool(name="ps_h", bufs=2))
        ps_y = ctx.enter_context(tc.psum_pool(name="ps_y", bufs=1))
        ctx.enter_context(tc.manual_schedule())

        ident = const.tile([P, P], F32, name="ident")
        ones = const.tile([P, P], BF16, name="ones")
        brow = const.tile([P, P], BF16, name="brow")
        warm = const.tile([P, 1], F32, name="warm")
        bias4 = const.tile([P, GROUP * P], F32, name="bias4")
        l_sb = const.tile([P, COLS], BF16, name="l_sb")
        r_sb = const.tile([P, 512], BF16, name="r_sb")
        r32 = const.tile([P, 512], F32, name="r32")
        r_grouped = const.tile([P, 512], BF16, name="r_grouped", align_bytes=64)
        r_codes = const.tile([P, P], U32, name="r_codes", align_bytes=64)
        r_scales = const.tile([P, P], U8, name="r_scales", align_bytes=64)
        l_codes = const.tile([P, 1024], U32, name="l_codes", align_bytes=64)
        l_scales = const.tile([P, 1024], U8, name="l_scales", align_bytes=64)

        x_tiles = {}

        def load_group(g):
            x_sb = xpool.tile([P, GROUP * COLS], BF16, name="x_sb")
            x_tiles[g] = x_sb
            for t in range(GROUP):
                nc.sync.dma_start(out=x_sb[:, t * COLS:(t + 1) * COLS], in_=xg[g, :, t, :])

        nc.vector.memset(brow[:], 0.0)
        nc.vector.memset(ones[:], 1.0)
        masks.make_identity(nc, ident[:])
        nc.scalar.dma_start(out=r_sb[:], in_=factorR[0])
        nc.scalar.dma_start(out=brow[0:1, :], in_=bias.rearrange("(o n) -> o n", o=1))
        nc.scalar.copy(out=warm[:], in_=ones[:, 0:1])
        for k in range(KB):
            nc.sync.dma_start(out=l_sb[:, k * 1024:(k + 1) * 1024], in_=factorL[k])
        for g in range(XBUFS):
            load_group(g)

        def copy_out(engine, dst_ap, src_ap):
            if engine == "S":
                nc.scalar.copy(out=dst_ap, in_=src_ap)
            else:
                nc.vector.tensor_copy(out=dst_ap, in_=src_ap)

        def bridge(bank):
            nc.tensor.matmul(bank[:, 0:32], lhsT=ones[:], rhs=ones[:, 0:32], start=True, stop=True)

        def transpose_block(words, grouped, k, engine, bridged=False):
            bank = ps_t.tile([P, 512], F32, name="bank")
            if bridged:
                bridge(bank)
            for g in range(2):
                for u in range(2):
                    src = k * 512 + g * 256 + u * P
                    dst = u * 256 + g * P
                    nc.tensor.transpose(bank[:, dst:dst + P], words[:, src:src + P], ident[:])
            copy_out(
                engine,
                grouped[:].bitcast(F32)[:, k * 512:(k + 1) * 512].rearrange("p (c u) -> p c u", u=2),
                bank[:].rearrange("p (u c) -> p c u", u=2),
            )

        def quantise(grouped, codes, scales, lo, hi):
            nc.vector.quantize_mx(
                out=codes[:, lo:hi].bitcast(FP8X4),
                scales=scales[:, lo:hi],
                in_=grouped[:, 4 * lo:4 * hi],
            )

        grouped_of = {}
        codes_of = {}
        h_bank_of = {}
        h_of = {}
        y_of = {}
        o_of = {}

        def stage_t(t, last_engine="S"):
            g, j = divmod(t, GROUP)
            words = x_tiles[g][:].bitcast(F32)[:, j * 2048:(j + 1) * 2048]
            grouped = gpool.tile([P, COLS], BF16, name="grouped", align_bytes=64)
            grouped_of[t] = grouped
            for k in range(KB):
                transpose_block(words, grouped, k, last_engine if k == KB - 1 else "S", k == 0 and t > M_LAG)
            if j == GROUP - 1 and g + XBUFS < NGROUPS:
                load_group(g + XBUFS)

        def stage_q(t, k0=0, k1=KB):
            if k0 == 0:
                codes = cpool.tile([P, 1024], U32, name="codes", align_bytes=64)
                scales = cpool.tile([P, 1024], U8, name="scales", align_bytes=64)
                codes_of[t] = (codes, scales)
            codes, scales = codes_of[t]
            quantise(grouped_of[t], codes, scales, k0 * 256, k1 * 256)

        def stage_m(t, k0=0, k1=KB, pool="h", bridged=False):
            codes, scales = codes_of[t]
            if k0 == 0 and pool == "h":
                h_bank_of[t] = ps_h.tile([P, 512], F32, name="h_bank")
            if k0 == 0 and pool == "t":
                h_bank_of[t] = ps_t.tile([P, 512], F32, name="bank")
            h_bank = h_bank_of[t]
            if bridged:
                bridge(h_bank)
            for k in range(k0, k1):
                for g in range(2):
                    c = k * 256 + g * P
                    nc.tensor.matmul_mx(
                        out=h_bank[:, k * P:(k + 1) * P],
                        lhsT=l_codes[:, c:c + P].bitcast(FP8X4),
                        lhsT_scale=l_scales[:, c:c + P],
                        rhs=codes[:, c:c + P].bitcast(FP8X4),
                        rhs_scale=scales[:, c:c + P],
                        start=(g == 0),
                        stop=(g == 1),
                    )

        def stage_he(t, engine):
            g, j = divmod(t, GROUP)
            if j == 0:
                h_grouped = hpool.tile([P, GROUP * 512], BF16, name="h_grouped", align_bytes=64)
                h_codes = hpool.tile([P, GROUP * P], U32, name="h_codes", align_bytes=64)
                h_scales = hpool.tile([P, GROUP * P], U8, name="h_scales", align_bytes=64)
                h_of[g] = (h_grouped, h_codes, h_scales)
            copy_out(
                engine,
                h_of[g][0][:, j * 512:(j + 1) * 512].rearrange("p (b k) -> p b k", k=KB),
                h_bank_of[t][:].rearrange("p (k b) -> p b k", k=KB),
            )

        def stage_hq(t, n):
            g, j = divmod(t, GROUP)
            h_grouped, h_codes, h_scales = h_of[g]
            quantise(h_grouped, h_codes, h_scales, j * P, (j + n) * P)

        def stage_y(t, n, pool):
            g, j = divmod(t, GROUP)
            h_grouped, h_codes, h_scales = h_of[g]
            if pool == "y":
                y_bank = ps_y.tile([P, 512], F32, name="y_bank")
            else:
                y_bank = ps_t.tile([P, 512], F32, name="bank")
            y_of[t] = y_bank
            for r in range(n):
                c = (j + r) * P
                nc.tensor.matmul_mx(
                    out=y_bank[:, r * P:(r + 1) * P],
                    lhsT=h_codes[:, c:c + P].bitcast(FP8X4),
                    lhsT_scale=h_scales[:, c:c + P],
                    rhs=r_codes[:].bitcast(FP8X4),
                    rhs_scale=r_scales[:],
                    start=True,
                    stop=True,
                )

        def stage_ye(t, n):
            g, j = divmod(t, GROUP)
            if j == 0:
                o_of[g] = opool.tile([P, GROUP * P], F32, name="o_sb")
            nc.vector.tensor_tensor(
                out=o_of[g][:, j * P:(j + n) * P],
                in0=y_of[t][:, 0:n * P],
                in1=bias4[:, 0:n * P],
                op=mybir.AluOpType.add,
            )

        def store(g, j0, j1):
            nc.sync.dma_start(out=og[g][:, j0 * P:j1 * P], in_=o_of[g][:, j0 * P:j1 * P])

        def small_operands_front():
            nc.vector.tensor_copy(out=r32[:], in_=r_sb[:])
            bias_ps = ps_t.tile([P, 512], F32, name="bank")
            nc.tensor.matmul(bias_ps[:, 0:P], lhsT=ones[:], rhs=brow[:], start=True, stop=True)
            nc.scalar.copy(
                out=bias4[:].rearrange("p (t s) -> p t s", t=GROUP),
                in_=bias_ps[:, 0:P].unsqueeze(1).to_broadcast([P, GROUP, P]),
            )
            r_ps = ps_t.tile([P, 512], F32, name="bank")
            for t in range(4):
                nc.tensor.transpose(r_ps[:, t * P:(t + 1) * P], r32[:, t * P:(t + 1) * P], ident[:])
            nc.vector.tensor_copy(
                out=r_grouped[:].rearrange("p (s t) -> p s t", t=4),
                in_=r_ps[:].rearrange("p (t s) -> p s t", t=4),
            )

        l_grouped = gpool.tile([P, COLS], BF16, name="grouped", align_bytes=64)
        for k in range(KB):
            transpose_block(l_sb[:].bitcast(F32), l_grouped, k, "S")
        quantise(l_grouped, l_codes, l_scales, 0, 1024)

        last = TILES - 1
        last_load_tile = (NGROUPS - XBUFS) * GROUP - 1
        ready_groups = []
        for i in range(last - 1):
            hq_group, hq_rest = divmod(i - M_LAG - (GROUP - 1), GROUP)
            y_group, y_rest = divmod(i - M_LAG - Y_LAG - (GROUP - 1), GROUP)
            do_hq = hq_rest == 0 and hq_group >= 0
            do_y = y_rest == 0 and y_group >= 0
            stage_t(i, "V" if (i % GROUP == V_SHARE and i < last - GROUP) else "S")
            if i == 1:
                small_operands_front()
            if i >= M_LAG:
                stage_m(i - M_LAG, bridged=True)
            if do_y:
                stage_y(y_group * GROUP, GROUP, "y")
            if i >= M_LAG:
                stage_he(i - M_LAG, "V")
            if do_y:
                stage_ye(y_group * GROUP, GROUP)
                ready_groups.append(y_group)
            if i >= last_load_tile:
                for g in ready_groups:
                    store(g, 0, GROUP)
                ready_groups = []
            stage_q(i)
            if i == 1:
                quantise(r_grouped, r_codes, r_scales, 0, P)
            if do_hq:
                stage_hq(hq_group * GROUP, GROUP)

        i = last - 1
        stage_t(i)
        stage_m(i - 2, bridged=True)
        stage_q(i, 0, 2)
        stage_he(i - 2, "V")
        stage_q(i, 2, 4)

        i = last
        stage_t(i)
        stage_m(i - 2, bridged=True)
        stage_y(i - 7, GROUP, "y")
        stage_he(i - 2, "S")
        stage_q(i, 0, 2)
        stage_m(i - 1)
        stage_he(i - 1, "S")
        stage_q(i, 2, 3)
        stage_q(i, 3, 4)
        stage_m(i, 0, 2, "t")
        stage_m(i, 2, 3, "t")
        stage_m(i, 3, 4, "t")
        stage_he(i, "S")
        stage_ye(i - 7, GROUP)
        store(NGROUPS - 2, 0, GROUP)
        stage_hq(i - 3, 2)
        stage_hq(i - 1, 1)
        stage_y(i - 3, 2, "t")
        stage_hq(i, 1)
        stage_ye(i - 3, 2)
        store(NGROUPS - 1, 0, 2)
        stage_y(i - 1, 2, "t")
        stage_ye(i - 1, 2)
        store(NGROUPS - 1, 2, GROUP)
